import numpy as np
import ml_dtypes


def mxq(x, axis, fmt="e4m3"):
    dtype, down = {"e4m3": (ml_dtypes.float8_e4m3fn, 7), "e5m2": (ml_dtypes.float8_e5m2, 14)}[fmt]
    v = np.moveaxis(np.asarray(x, np.float32).astype(ml_dtypes.bfloat16).astype(np.float64), axis, -1)
    blocks = v.reshape(v.shape[:-1] + (-1, 32))
    amax = np.abs(blocks).max(-1, keepdims=True)
    byte = np.maximum(np.where(amax > 0, np.frexp(amax)[1] - 1 + 127, 0) - down, 1)
    scale = np.exp2(byte - 127.0)
    codes = (blocks / scale).astype(np.float32).astype(dtype).astype(np.float64)
    return np.moveaxis((codes * scale).reshape(v.shape), -1, axis)


WIDE = False


def mx_kscale(k):
    if not WIDE:
        return np.ones(k)
    levels = np.array([10, -10, 5, -5, 0])
    a = np.random.permutation(np.resize(levels, k // 512 * 4)).reshape(k // 512, 4)
    idx = np.arange(k)
    return np.exp2(a[idx // 512, idx % 128 // 32])


BF16 = ml_dtypes.bfloat16


def bf(x):
    return np.asarray(x, np.float32).astype(BF16)


def f64(x):
    return np.asarray(x).astype(np.float64)


B, S, IN_DIM, OUT_DIM, MOD_DIM = 4, 64, 8192, 1024, 512
EPS = 1e-8
GAIN = np.sqrt(2.0 / (1.0 + 0.2 ** 2))


def setup_inputs():
    ks = mx_kscale(MOD_DIM)
    kt = mx_kscale(IN_DIM)
    return {"x": bf(np.random.standard_normal((B, S, IN_DIM))),
            "modulation": bf(np.random.standard_normal((B, S, MOD_DIM)) * ks),
            "weight": bf(np.random.standard_normal((OUT_DIM, IN_DIM)) * GAIN / np.sqrt(IN_DIM) / kt[None, :]),
            "bias": bf(np.random.standard_normal(OUT_DIM) * 0.1),
            "mod_w": bf(np.random.standard_normal((IN_DIM, MOD_DIM)) / np.sqrt(MOD_DIM) * kt[:, None] / ks[None, :]),
            "mod_b": bf((1.0 + 0.1 * np.random.standard_normal(IN_DIM)) * kt)}


def reference(x, modulation, weight, bias, mod_w, mod_b):
    xf, w = f64(x), f64(weight)
    s = (mxq(f64(modulation), 2, "e4m3") @ mxq(f64(mod_w), 1, "e4m3").T) + f64(mod_b)
    out = mxq(xf * s, 2, "e4m3") @ mxq(w, 1, "e4m3").T
    demod = 1.0 / np.sqrt((mxq(s * s, 2, "e4m3") @ mxq(w * w, 1, "e4m3").T) + EPS)
    return out * demod + f64(bias)

@@ -1,0 +1,315 @@
+from contextlib import ExitStack
+
+import concourse.mybir as mybir
+from concourse.masks import make_identity
+
+F32 = mybir.dt.float32
+BF16 = mybir.dt.bfloat16
+U32 = mybir.dt.uint32
+U8 = mybir.dt.uint8
+FP8X4 = mybir.dt.float8_e4m3fn_x4
+ACT = mybir.ActivationFunctionType
+ALU = mybir.AluOpType
+
+P = 128
+TOKENS = 256
+IN_DIM = 8192
+OUT_DIM = 1024
+MOD_DIM = 512
+EPS = 1e-8
+
+K_PASS = 512
+PASSES = IN_DIM // K_PASS
+WORDS = K_PASS // 2
+BANK = 512
+TOKEN_TILES = TOKENS // P
+OUT_HALF = 512
+HALVES = OUT_DIM // OUT_HALF
+ROW_TILES = OUT_HALF // P
+
+MW_LOAD_PASSES = 2
+X_LOAD_PASSES = 4
+W_LOAD_PASSES = 4
+S_QUANT_PASSES = 2
+W_BATCH_PASSES = 2
+
+W_BATCH_COLS = W_BATCH_PASSES * OUT_HALF * 4
+SQUARE_COLS_VECTOR = 2688
+
+FLOPS = 2 * TOKENS * (MOD_DIM * IN_DIM + 2 * IN_DIM * OUT_DIM)
+
+
+def transpose_words(nc, bank_cols, rows_bf16, first_word, ident):
+    nc.tensor.transpose(
+        bank_cols, rows_bf16.bitcast(F32)[:, first_word : first_word + P], ident
+    )
+
+
+def tile_modulatedlinear_k_kernel(tc, x, modulation, weight, bias, mod_w, mod_b, out):
+    nc = tc.nc
+    x_rows = x.flatten_outer_dims().rearrange("(a r) i -> r a i", r=P)
+    modulation_rows = modulation.flatten_outer_dims().rearrange("(a r) k -> r a k", r=P)
+    out_rows = out.flatten_outer_dims()
+    mod_w_rows = mod_w.rearrange("(c r e) k -> r c e k", r=P, e=2)
+    weight_rows = weight.rearrange("(h b r) i -> r h b i", b=ROW_TILES, r=P)
+
+    with ExitStack() as whole:
+        const = whole.enter_context(tc.tile_pool(name="const", bufs=1))
+        w_in = whole.enter_context(tc.tile_pool(name="w_in", bufs=3))
+
+        ident = const.tile([P, P], F32)
+        make_identity(nc, ident[:])
+        eps = const.tile([P, 1], F32)
+        nc.vector.memset(eps[:], EPS)
+        table_warm = const.tile([P, 1], F32)
+        nc.scalar.activation(out=table_warm[:], in_=eps[:], func=ACT.Abs_reciprocal_sqrt)
+
+        bias_all = const.tile([P, OUT_DIM], BF16)
+        nc.gpsimd.dma_start(out=bias_all[:], in_=bias.partition_broadcast(P))
+
+        xs_codes = const.tile([P, PASSES * TOKENS], U32, align_bytes=64)
+        xs_scales = const.tile([P, PASSES * TOKENS], U8, align_bytes=64)
+        ss_codes = const.tile([P, PASSES * TOKENS], U32, align_bytes=64)
+        ss_scales = const.tile([P, PASSES * TOKENS], U8, align_bytes=64)
+        mod_b_cols = const.tile([P, 4 * PASSES], F32)
+
+        with ExitStack() as stage1:
+            once = stage1.enter_context(tc.tile_pool(name="once", bufs=1))
+            loads = stage1.enter_context(tc.tile_pool(name="loads", bufs=3))
+            work = stage1.enter_context(tc.tile_pool(name="work", bufs=3))
+            pairs = stage1.enter_context(tc.tile_pool(name="pairs", bufs=2))
+            turned = stage1.enter_context(tc.psum_pool(name="turned", bufs=3))
+            turned_x = stage1.enter_context(tc.psum_pool(name="turned_x", bufs=2))
+            s_psum = stage1.enter_context(tc.psum_pool(name="s_psum", bufs=3))
+
+            mod_raw = once.tile([P, TOKEN_TILES, MOD_DIM], BF16)
+            nc.sync.dma_start(out=mod_raw[:], in_=modulation_rows)
+            mod_bank = turned.tile([P, BANK], F32, tag="bank")
+            for u in range(2):
+                for a in range(TOKEN_TILES):
+                    transpose_words(
+                        nc, mod_bank[:, (u * TOKEN_TILES + a) * P : (u * TOKEN_TILES + a + 1) * P],
+                        mod_raw[:, a, :], u * P, ident[:],
+                    )
+            mod_grouped = once.tile([P, TOKENS * 4], BF16, align_bytes=64)
+            nc.scalar.copy(
+                out=mod_grouped[:].bitcast(F32).rearrange("p (t u) -> p t u", u=2),
+                in_=mod_bank[:].rearrange("p (u t) -> p t u", u=2),
+            )
+            mod_codes = once.tile([P, TOKENS], U32, align_bytes=64)
+            mod_scales = once.tile([P, TOKENS], U8, align_bytes=64)
+            nc.vector.quantize_mx(
+                out=mod_codes[:].bitcast(FP8X4), scales=mod_scales[:], in_=mod_grouped[:]
+            )
+
+            mod_b_raw = once.tile([P, 2 * P], BF16)
+            nc.vector.memset(mod_b_raw[:], 0.0)
+            nc.sync.dma_start(
+                out=mod_b_raw[: 2 * PASSES, :], in_=mod_b.rearrange("(c w) -> c w", w=2 * P)
+            )
+            mod_b_bank = turned.tile([P, BANK], F32, tag="bank")
+            transpose_words(nc, mod_b_bank[:, :P], mod_b_raw[:], 0, ident[:])
+            nc.vector.tensor_copy(
+                out=mod_b_cols[:], in_=mod_b_bank[:, : 2 * PASSES].bitcast(BF16)
+            )
+
+            for g in range(PASSES):
+                if g % MW_LOAD_PASSES == 0:
+                    mw_raw = loads.tile([P, 2 * MW_LOAD_PASSES, 2, MOD_DIM], BF16)
+                    nc.sync.dma_start(
+                        out=mw_raw[:], in_=mod_w_rows[:, 2 * g : 2 * (g + MW_LOAD_PASSES), :, :]
+                    )
+                if g % X_LOAD_PASSES == 0:
+                    x_raw = loads.tile([P, TOKEN_TILES, X_LOAD_PASSES * K_PASS], BF16)
+                    nc.sync.dma_start(
+                        out=x_raw[:], in_=x_rows[:, :, g * K_PASS : (g + X_LOAD_PASSES) * K_PASS]
+                    )
+
+                mw_grouped = work.tile([P, 4 * P * 4], BF16, align_bytes=64)
+                mw_words = mw_grouped[:].bitcast(F32).rearrange(
+                    "p (u e r v) -> p u e r v", u=2, e=2, v=2
+                )
+                for u in range(2):
+                    c = 2 * (g % MW_LOAD_PASSES) + u
+                    mw_bank = turned.tile([P, BANK], F32, tag="bank")
+                    for e in range(2):
+                        for v in range(2):
+                            transpose_words(
+                                nc, mw_bank[:, (2 * e + v) * P : (2 * e + v + 1) * P],
+                                mw_raw[:, c, e, :], v * P, ident[:],
+                            )
+                    nc.scalar.copy(
+                        out=mw_words[:, u],
+                        in_=mw_bank[:].rearrange("p (e v r) -> p e r v", e=2, v=2),
+                    )
+                mw_codes = work.tile([P, 4 * P], U32, align_bytes=64)
+                mw_scales = work.tile([P, 4 * P], U8, align_bytes=64)
+                nc.vector.quantize_mx(
+                    out=mw_codes[:].bitcast(FP8X4), scales=mw_scales[:], in_=mw_grouped[:]
+                )
+
+                x_bank = turned_x.tile([P, BANK], F32)
+                for u in range(2):
+                    for a in range(TOKEN_TILES):
+                        transpose_words(
+                            nc, x_bank[:, (u * TOKEN_TILES + a) * P : (u * TOKEN_TILES + a + 1) * P],
+                            x_raw[:, a, :], (g % X_LOAD_PASSES) * WORDS + u * P, ident[:],
+                        )
+
+                s_sb = work.tile([P, 4 * TOKENS], F32)
+                for u in range(2):
+                    s_bank = s_psum.tile([P, BANK], F32)
+                    for e in range(2):
+                        j = 2 * u + e
+                        nc.tensor.matmul_mx(
+                            out=s_bank[:, e * TOKENS : (e + 1) * TOKENS],
+                            lhsT=mw_codes[:, j * P : (j + 1) * P].bitcast(FP8X4),
+                            lhsT_scale=mw_scales[:, j * P : (j + 1) * P],
+                            rhs=mod_codes[:].bitcast(FP8X4),
+                            rhs_scale=mod_scales[:],
+                            start=True,
+                            stop=True,
+                        )
+                    nc.vector.tensor_tensor(
+                        out=s_sb[:, u * BANK : (u + 1) * BANK].rearrange("p (t e) -> p t e", e=2),
+                        in0=s_bank[:].rearrange("p (e t) -> p t e", e=2),
+                        in1=mod_b_cols[:, 4 * g + 2 * u : 4 * g + 2 * u + 2]
+                        .unsqueeze(1)
+                        .to_broadcast([P, TOKENS, 2]),
+                        op=ALU.add,
+                    )
+
+                if g % S_QUANT_PASSES == 0:
+                    xs_grouped = pairs.tile([P, S_QUANT_PASSES * TOKENS * 4], BF16, align_bytes=64)
+                    ss_grouped = pairs.tile([P, S_QUANT_PASSES * TOKENS * 4], BF16, align_bytes=64)
+                cols = slice((g % S_QUANT_PASSES) * TOKENS * 4, (g % S_QUANT_PASSES + 1) * TOKENS * 4)
+                s_view = s_sb[:].rearrange("p (u t e) -> p t u e", u=2, e=2)
+                nc.vector.tensor_tensor(
+                    out=xs_grouped[:, cols].rearrange("p (t u e) -> p t u e", u=2, e=2),
+                    in0=x_bank[:].bitcast(BF16).rearrange("p (u t e) -> p t u e", u=2, e=2),
+                    in1=s_view,
+                    op=ALU.mult,
+                )
+                nc.scalar.activation(
+                    out=ss_grouped[:, cols].rearrange("p (t u e) -> p t u e", u=2, e=2),
+                    in_=s_view,
+                    func=ACT.Square,
+                )
+                if g % S_QUANT_PASSES == S_QUANT_PASSES - 1:
+                    kept = slice((g + 1 - S_QUANT_PASSES) * TOKENS, (g + 1) * TOKENS)
+                    nc.vector.quantize_mx(
+                        out=xs_codes[:, kept].bitcast(FP8X4), scales=xs_scales[:, kept],
+                        in_=xs_grouped[:],
+                    )
+                    nc.vector.quantize_mx(
+                        out=ss_codes[:, kept].bitcast(FP8X4), scales=ss_scales[:, kept],
+                        in_=ss_grouped[:],
+                    )
+
+        with ExitStack() as stage2:
+            w_work = stage2.enter_context(tc.tile_pool(name="w_work", bufs=3, reuse_waits="tile"))
+            tail = stage2.enter_context(tc.tile_pool(name="tail", bufs=2, reuse_waits="tile"))
+            w_turned = stage2.enter_context(tc.psum_pool(name="w_turned", bufs=4, reuse_waits="tile"))
+            sums = stage2.enter_context(tc.psum_pool(name="sums", bufs=1, reuse_waits="tile"))
+
+            for h in range(HALVES):
+                y_sums = []
+                q_sums = []
+                for a in range(TOKEN_TILES):
+                    y_bank = sums.tile([P, BANK], F32, name="y_bank%d" % a)
+                    q_bank = sums.tile([P, BANK], F32, name="q_bank%d" % a)
+                    y_sums.append(y_bank)
+                    q_sums.append(q_bank)
+
+                for g0 in range(0, PASSES, W_BATCH_PASSES):
+                    if g0 % W_LOAD_PASSES == 0:
+                        w_raw = w_in.tile([P, ROW_TILES, W_LOAD_PASSES * K_PASS], BF16)
+                        nc.sync.dma_start(
+                            out=w_raw[:],
+                            in_=weight_rows[:, h, :, g0 * K_PASS : (g0 + W_LOAD_PASSES) * K_PASS],
+                        )
+
+                    w_grouped = w_work.tile([P, W_BATCH_COLS], BF16, align_bytes=64)
+                    w_words = w_grouped[:].bitcast(F32).rearrange(
+                        "p (g n o u) -> p g n o u", g=W_BATCH_PASSES, n=2, u=2
+                    )
+                    for gl in range(W_BATCH_PASSES):
+                        for n in range(2):
+                            w_bank = w_turned.tile([P, BANK], F32)
+                            for u in range(2):
+                                for b in range(2):
+                                    transpose_words(
+                                        nc, w_bank[:, (2 * u + b) * P : (2 * u + b + 1) * P],
+                                        w_raw[:, 2 * n + b, :],
+                                        ((g0 + gl) % W_LOAD_PASSES) * WORDS + u * P, ident[:],
+                                    )
+                            nc.scalar.copy(
+                                out=w_words[:, gl, n],
+                                in_=w_bank[:].rearrange("p (u o) -> p o u", u=2),
+                            )
+                    w_squared = w_work.tile([P, W_BATCH_COLS], BF16, align_bytes=64)
+                    nc.vector.tensor_tensor(
+                        out=w_squared[:, :SQUARE_COLS_VECTOR],
+                        in0=w_grouped[:, :SQUARE_COLS_VECTOR],
+                        in1=w_grouped[:, :SQUARE_COLS_VECTOR],
+                        op=ALU.mult,
+                    )
+                    nc.scalar.activation(
+                        out=w_squared[:, SQUARE_COLS_VECTOR:],
+                        in_=w_grouped[:, SQUARE_COLS_VECTOR:],
+                        func=ACT.Square,
+                    )
+                    w_codes = w_work.tile([P, W_BATCH_COLS // 4], U32, align_bytes=64)
+                    w_scales = w_work.tile([P, W_BATCH_COLS // 4], U8, align_bytes=64)
+                    nc.vector.quantize_mx(
+                        out=w_codes[:].bitcast(FP8X4), scales=w_scales[:], in_=w_grouped[:]
+                    )
+                    w2_codes = w_work.tile([P, W_BATCH_COLS // 4], U32, align_bytes=64)
+                    w2_scales = w_work.tile([P, W_BATCH_COLS // 4], U8, align_bytes=64)
+                    nc.vector.quantize_mx(
+                        out=w2_codes[:].bitcast(FP8X4), scales=w2_scales[:], in_=w_squared[:]
+                    )
+
+                    for gl in range(W_BATCH_PASSES):
+                        g = g0 + gl
+                        moving = slice(gl * OUT_HALF, (gl + 1) * OUT_HALF)
+                        for a in range(TOKEN_TILES):
+                            still = slice(g * TOKENS + a * P, g * TOKENS + (a + 1) * P)
+                            nc.tensor.matmul_mx(
+                                out=q_sums[a][:],
+                                lhsT=ss_codes[:, still].bitcast(FP8X4),
+                                lhsT_scale=ss_scales[:, still],
+                                rhs=w2_codes[:, moving].bitcast(FP8X4),
+                                rhs_scale=w2_scales[:, moving],
+                                start=(g == 0),
+                                stop=(g == PASSES - 1),
+                            )
+                        for a in range(TOKEN_TILES):
+                            still = slice(g * TOKENS + a * P, g * TOKENS + (a + 1) * P)
+                            nc.tensor.matmul_mx(
+                                out=y_sums[a][:],
+                                lhsT=xs_codes[:, still].bitcast(FP8X4),
+                                lhsT_scale=xs_scales[:, still],
+                                rhs=w_codes[:, moving].bitcast(FP8X4),
+                                rhs_scale=w_scales[:, moving],
+                                start=(g == 0),
+                                stop=(g == PASSES - 1),
+                            )
+
+                for a in range(TOKEN_TILES):
+                    demod = tail.tile([P, OUT_HALF], F32)
+                    nc.scalar.activation(
+                        out=demod[:], in_=q_sums[a][:], func=ACT.Abs_reciprocal_sqrt, bias=eps[:]
+                    )
+                    result = tail.tile([P, OUT_HALF], F32)
+                    nc.vector.tensor_tensor(
+                        out=result[:], in0=y_sums[a][:], in1=demod[:], op=ALU.mult
+                    )
+                    nc.vector.tensor_tensor(
+                        out=result[:], in0=result[:],
+                        in1=bias_all[:, h * OUT_HALF : (h + 1) * OUT_HALF], op=ALU.add,
+                    )
+                    nc.sync.dma_start(
+                        out=out_rows[a * P : (a + 1) * P, h * OUT_HALF : (h + 1) * OUT_HALF],
+                        in_=result[:],
+                    )

@@ -23,18 +23,22 @@ PASSES = IN_DIM // K_PASS
 WORDS = K_PASS // 2
 BANK = 512
 TOKEN_TILES = TOKENS // P
-OUT_HALF = 512
-HALVES = OUT_DIM // OUT_HALF
-ROW_TILES = OUT_HALF // P
+ROUND_OUT = 512
+ROUNDS = OUT_DIM // ROUND_OUT
+ROW_TILES = ROUND_OUT // P
+W_PASSES = ROUNDS * PASSES
 
-MW_LOAD_PASSES = 2
-X_LOAD_PASSES = 4
-W_LOAD_PASSES = 4
-S_QUANT_PASSES = 2
-W_BATCH_PASSES = 2
+MW_LOAD = 2
+X_LOAD = 4
+W_LOAD = 4
+PAIR = 2
+PAIR_COLS = PAIR * ROUND_OUT * 4
+W_PAIRS = W_PASSES // PAIR
+ROUND_PAIRS = PASSES // PAIR
+W_EARLY = PASSES + 2
+KEPT_PAIRS = W_EARLY // PAIR
 
-W_BATCH_COLS = W_BATCH_PASSES * OUT_HALF * 4
-SQUARE_COLS_VECTOR = 2688
+SQUARE_COLS_VECTOR = 1920
 
 FLOPS = 2 * TOKENS * (MOD_DIM * IN_DIM + 2 * IN_DIM * OUT_DIM)
 
@@ -54,8 +58,11 @@ def tile_modulatedlinear_k_kernel(tc, x, modulation, weight, bias, mod_w, mod_b,
     weight_rows = weight.rearrange("(h b r) i -> r h b i", b=ROW_TILES, r=P)
 
     with ExitStack() as whole:
+        whole.enter_context(tc.manual_schedule())
         const = whole.enter_context(tc.tile_pool(name="const", bufs=1))
-        w_in = whole.enter_context(tc.tile_pool(name="w_in", bufs=3))
+        w_in = whole.enter_context(tc.tile_pool(name="w_in", bufs=2))
+        w_kept = whole.enter_context(tc.tile_pool(name="w_kept", bufs=KEPT_PAIRS))
+        w_turned = whole.enter_context(tc.psum_pool(name="w_turned", bufs=2))
 
         ident = const.tile([P, P], F32)
         make_identity(nc, ident[:])
@@ -73,17 +80,177 @@ def tile_modulatedlinear_k_kernel(tc, x, modulation, weight, bias, mod_w, mod_b,
         ss_scales = const.tile([P, PASSES * TOKENS], U8, align_bytes=64)
         mod_b_cols = const.tile([P, 4 * PASSES], F32)
 
+        w_raw = {}
+        w_grouped = {}
+
+        def load_weight(load):
+            first = load * W_LOAD
+            raw = w_in.tile([P, ROW_TILES, W_LOAD * K_PASS], BF16, name="w_raw")
+            nc.sync.dma_start(
+                out=raw[:],
+                in_=weight_rows[
+                    :, first // PASSES, :,
+                    (first % PASSES) * K_PASS : (first % PASSES + W_LOAD) * K_PASS,
+                ],
+            )
+            w_raw[load] = raw
+
+        def turn_weight(w):
+            if w % PAIR == 0:
+                grouped = w_kept.tile([P, PAIR_COLS], BF16, align_bytes=64, name="w_grouped")
+                w_grouped[w // PAIR] = grouped
+            words = w_grouped[w // PAIR][:].bitcast(F32).rearrange(
+                "p (g n o u) -> p g n o u", g=PAIR, n=2, u=2
+            )
+            for n in range(2):
+                w_bank = w_turned.tile([P, BANK], F32)
+                for u in range(2):
+                    for b in range(2):
+                        transpose_words(
+                            nc, w_bank[:, (2 * u + b) * P : (2 * u + b + 1) * P],
+                            w_raw[w // W_LOAD][:, 2 * n + b, :],
+                            (w % W_LOAD) * WORDS + u * P, ident[:],
+                        )
+                nc.scalar.copy(
+                    out=words[:, w % PAIR, n], in_=w_bank[:].rearrange("p (u o) -> p o u", u=2)
+                )
+
         with ExitStack() as stage1:
             once = stage1.enter_context(tc.tile_pool(name="once", bufs=1))
-            loads = stage1.enter_context(tc.tile_pool(name="loads", bufs=3))
-            work = stage1.enter_context(tc.tile_pool(name="work", bufs=3))
-            pairs = stage1.enter_context(tc.tile_pool(name="pairs", bufs=2))
-            turned = stage1.enter_context(tc.psum_pool(name="turned", bufs=3))
+            loads = stage1.enter_context(tc.tile_pool(name="loads", bufs=2))
+            work = stage1.enter_context(tc.tile_pool(name="work", bufs=2))
+            turned = stage1.enter_context(tc.psum_pool(name="turned", bufs=2))
             turned_x = stage1.enter_context(tc.psum_pool(name="turned_x", bufs=2))
-            s_psum = stage1.enter_context(tc.psum_pool(name="s_psum", bufs=3))
+            s_psum = stage1.enter_context(tc.psum_pool(name="s_psum", bufs=2))
+
+            mw_raw = {}
+            x_raw = {}
+            mw_grouped = {}
+            mw_codes = {}
+            mw_scales = {}
+            x_banks = {}
+            s_values = {}
+            xs_grouped = {}
+            ss_grouped = {}
+
+            def load_mod_w(load):
+                raw = loads.tile([P, 2 * MW_LOAD, 2, MOD_DIM], BF16, name="mw_raw")
+                nc.sync.dma_start(
+                    out=raw[:],
+                    in_=mod_w_rows[:, 2 * MW_LOAD * load : 2 * MW_LOAD * (load + 1), :, :],
+                )
+                mw_raw[load] = raw
+
+            def load_x(load):
+                raw = loads.tile([P, TOKEN_TILES, X_LOAD * K_PASS], BF16, name="x_raw")
+                nc.sync.dma_start(
+                    out=raw[:],
+                    in_=x_rows[:, :, load * X_LOAD * K_PASS : (load + 1) * X_LOAD * K_PASS],
+                )
+                x_raw[load] = raw
+
+            def turn_mod_w(g):
+                grouped = work.tile([P, 4 * P * 4], BF16, align_bytes=64, name="mw_grouped")
+                words = grouped[:].bitcast(F32).rearrange("p (u e r v) -> p u e r v", u=2, e=2, v=2)
+                for u in range(2):
+                    mw_bank = turned.tile([P, BANK], F32, tag="bank")
+                    for e in range(2):
+                        for v in range(2):
+                            transpose_words(
+                                nc, mw_bank[:, (2 * e + v) * P : (2 * e + v + 1) * P],
+                                mw_raw[g // MW_LOAD][:, 2 * (g % MW_LOAD) + u, e, :], v * P, ident[:],
+                            )
+                    nc.scalar.copy(
+                        out=words[:, u], in_=mw_bank[:].rearrange("p (e v r) -> p e r v", e=2, v=2)
+                    )
+                mw_grouped[g] = grouped
+
+            def quantise_mod_w(g):
+                codes = work.tile([P, 4 * P], U32, align_bytes=64, name="mw_codes")
+                scales = work.tile([P, 4 * P], U8, align_bytes=64, name="mw_scales")
+                nc.vector.quantize_mx(
+                    out=codes[:].bitcast(FP8X4), scales=scales[:], in_=mw_grouped[g][:]
+                )
+                mw_codes[g] = codes
+                mw_scales[g] = scales
+
+            def first_matmul(g):
+                x_bank = turned_x.tile([P, BANK], F32)
+                for u in range(2):
+                    for a in range(TOKEN_TILES):
+                        transpose_words(
+                            nc, x_bank[:, (u * TOKEN_TILES + a) * P : (u * TOKEN_TILES + a + 1) * P],
+                            x_raw[g // X_LOAD][:, a, :], (g % X_LOAD) * WORDS + u * P, ident[:],
+                        )
+                x_banks[g] = x_bank
+                s_sb = work.tile([P, 4 * TOKENS], F32)
+                s_halves = []
+                for u in range(2):
+                    s_bank = s_psum.tile([P, BANK], F32)
+                    for e in range(2):
+                        j = 2 * u + e
+                        nc.tensor.matmul_mx(
+                            out=s_bank[:, e * TOKENS : (e + 1) * TOKENS],
+                            lhsT=mw_codes[g][:, j * P : (j + 1) * P].bitcast(FP8X4),
+                            lhsT_scale=mw_scales[g][:, j * P : (j + 1) * P],
+                            rhs=mod_codes[:].bitcast(FP8X4),
+                            rhs_scale=mod_scales[:],
+                            start=True,
+                            stop=True,
+                        )
+                    s_halves.append(s_bank)
+                for u in range(2):
+                    nc.vector.tensor_tensor(
+                        out=s_sb[:, u * BANK : (u + 1) * BANK].rearrange("p (t e) -> p t e", e=2),
+                        in0=s_halves[u][:].rearrange("p (e t) -> p t e", e=2),
+                        in1=mod_b_cols[:, 4 * g + 2 * u : 4 * g + 2 * u + 2]
+                        .unsqueeze(1)
+                        .to_broadcast([P, TOKENS, 2]),
+                        op=ALU.add,
+                    )
+                s_values[g] = s_sb
+
+            def products(g):
+                if g % PAIR == 0:
+                    xs_pair = work.tile([P, PAIR * TOKENS * 4], BF16, align_bytes=64, name="xs_grouped")
+                    ss_pair = work.tile([P, PAIR * TOKENS * 4], BF16, align_bytes=64, name="ss_grouped")
+                    xs_grouped[g // PAIR] = xs_pair
+                    ss_grouped[g // PAIR] = ss_pair
+                cols = slice((g % PAIR) * TOKENS * 4, (g % PAIR + 1) * TOKENS * 4)
+                s_view = s_values[g][:].rearrange("p (u t e) -> p t u e", u=2, e=2)
+                nc.vector.tensor_tensor(
+                    out=xs_grouped[g // PAIR][:, cols].rearrange("p (t u e) -> p t u e", u=2, e=2),
+                    in0=x_banks[g][:].bitcast(BF16).rearrange("p (u t e) -> p t u e", u=2, e=2),
+                    in1=s_view,
+                    op=ALU.mult,
+                )
+                nc.scalar.activation(
+                    out=ss_grouped[g // PAIR][:, cols].rearrange("p (t u e) -> p t u e", u=2, e=2),
+                    in_=s_view,
+                    func=ACT.Square,
+                )
+
+            def quantise_products(pair):
+                kept = slice(pair * PAIR * TOKENS, (pair + 1) * PAIR * TOKENS)
+                nc.vector.quantize_mx(
+                    out=xs_codes[:, kept].bitcast(FP8X4), scales=xs_scales[:, kept],
+                    in_=xs_grouped[pair][:],
+                )
+                nc.vector.quantize_mx(
+                    out=ss_codes[:, kept].bitcast(FP8X4), scales=ss_scales[:, kept],
+                    in_=ss_grouped[pair][:],
+                )
 
             mod_raw = once.tile([P, TOKEN_TILES, MOD_DIM], BF16)
             nc.sync.dma_start(out=mod_raw[:], in_=modulation_rows)
+            load_mod_w(0)
+            mod_b_raw = once.tile([P, 2 * P], BF16)
+            nc.vector.memset(mod_b_raw[:], 0.0)
+            nc.sync.dma_start(
+                out=mod_b_raw[: 2 * PASSES, :], in_=mod_b.rearrange("(c w) -> c w", w=2 * P)
+            )
+            load_x(0)
+
             mod_bank = turned.tile([P, BANK], F32, tag="bank")
             for u in range(2):
                 for a in range(TOKEN_TILES):
@@ -102,214 +269,132 @@ def tile_modulatedlinear_k_kernel(tc, x, modulation, weight, bias, mod_w, mod_b,
                 out=mod_codes[:].bitcast(FP8X4), scales=mod_scales[:], in_=mod_grouped[:]
             )
 
-            mod_b_raw = once.tile([P, 2 * P], BF16)
-            nc.vector.memset(mod_b_raw[:], 0.0)
-            nc.sync.dma_start(
-                out=mod_b_raw[: 2 * PASSES, :], in_=mod_b.rearrange("(c w) -> c w", w=2 * P)
-            )
             mod_b_bank = turned.tile([P, BANK], F32, tag="bank")
             transpose_words(nc, mod_b_bank[:, :P], mod_b_raw[:], 0, ident[:])
-            nc.vector.tensor_copy(
-                out=mod_b_cols[:], in_=mod_b_bank[:, : 2 * PASSES].bitcast(BF16)
-            )
+            nc.vector.tensor_copy(out=mod_b_cols[:], in_=mod_b_bank[:, : 2 * PASSES].bitcast(BF16))
 
-            for g in range(PASSES):
-                if g % MW_LOAD_PASSES == 0:
-                    mw_raw = loads.tile([P, 2 * MW_LOAD_PASSES, 2, MOD_DIM], BF16)
-                    nc.sync.dma_start(
-                        out=mw_raw[:], in_=mod_w_rows[:, 2 * g : 2 * (g + MW_LOAD_PASSES), :, :]
-                    )
-                if g % X_LOAD_PASSES == 0:
-                    x_raw = loads.tile([P, TOKEN_TILES, X_LOAD_PASSES * K_PASS], BF16)
-                    nc.sync.dma_start(
-                        out=x_raw[:], in_=x_rows[:, :, g * K_PASS : (g + X_LOAD_PASSES) * K_PASS]
-                    )
-
-                mw_grouped = work.tile([P, 4 * P * 4], BF16, align_bytes=64)
-                mw_words = mw_grouped[:].bitcast(F32).rearrange(
-                    "p (u e r v) -> p u e r v", u=2, e=2, v=2
-                )
-                for u in range(2):
-                    c = 2 * (g % MW_LOAD_PASSES) + u
-                    mw_bank = turned.tile([P, BANK], F32, tag="bank")
-                    for e in range(2):
-                        for v in range(2):
-                            transpose_words(
-                                nc, mw_bank[:, (2 * e + v) * P : (2 * e + v + 1) * P],
-                                mw_raw[:, c, e, :], v * P, ident[:],
-                            )
-                    nc.scalar.copy(
-                        out=mw_words[:, u],
-                        in_=mw_bank[:].rearrange("p (e v r) -> p e r v", e=2, v=2),
-                    )
-                mw_codes = work.tile([P, 4 * P], U32, align_bytes=64)
-                mw_scales = work.tile([P, 4 * P], U8, align_bytes=64)
-                nc.vector.quantize_mx(
-                    out=mw_codes[:].bitcast(FP8X4), scales=mw_scales[:], in_=mw_grouped[:]
-                )
-
-                x_bank = turned_x.tile([P, BANK], F32)
-                for u in range(2):
-                    for a in range(TOKEN_TILES):
-                        transpose_words(
-                            nc, x_bank[:, (u * TOKEN_TILES + a) * P : (u * TOKEN_TILES + a + 1) * P],
-                            x_raw[:, a, :], (g % X_LOAD_PASSES) * WORDS + u * P, ident[:],
-                        )
-
-                s_sb = work.tile([P, 4 * TOKENS], F32)
-                for u in range(2):
-                    s_bank = s_psum.tile([P, BANK], F32)
-                    for e in range(2):
-                        j = 2 * u + e
-                        nc.tensor.matmul_mx(
-                            out=s_bank[:, e * TOKENS : (e + 1) * TOKENS],
-                            lhsT=mw_codes[:, j * P : (j + 1) * P].bitcast(FP8X4),
-                            lhsT_scale=mw_scales[:, j * P : (j + 1) * P],
-                            rhs=mod_codes[:].bitcast(FP8X4),
-                            rhs_scale=mod_scales[:],
-                            start=True,
-                            stop=True,
-                        )
-                    nc.vector.tensor_tensor(
-                        out=s_sb[:, u * BANK : (u + 1) * BANK].rearrange("p (t e) -> p t e", e=2),
-                        in0=s_bank[:].rearrange("p (e t) -> p t e", e=2),
-                        in1=mod_b_cols[:, 4 * g + 2 * u : 4 * g + 2 * u + 2]
-                        .unsqueeze(1)
-                        .to_broadcast([P, TOKENS, 2]),
-                        op=ALU.add,
-                    )
-
-                if g % S_QUANT_PASSES == 0:
-                    xs_grouped = pairs.tile([P, S_QUANT_PASSES * TOKENS * 4], BF16, align_bytes=64)
-                    ss_grouped = pairs.tile([P, S_QUANT_PASSES * TOKENS * 4], BF16, align_bytes=64)
-                cols = slice((g % S_QUANT_PASSES) * TOKENS * 4, (g % S_QUANT_PASSES + 1) * TOKENS * 4)
-                s_view = s_sb[:].rearrange("p (u t e) -> p t u e", u=2, e=2)
-                nc.vector.tensor_tensor(
-                    out=xs_grouped[:, cols].rearrange("p (t u e) -> p t u e", u=2, e=2),
-                    in0=x_bank[:].bitcast(BF16).rearrange("p (u t e) -> p t u e", u=2, e=2),
-                    in1=s_view,
-                    op=ALU.mult,
-                )
-                nc.scalar.activation(
-                    out=ss_grouped[:, cols].rearrange("p (t u e) -> p t u e", u=2, e=2),
-                    in_=s_view,
-                    func=ACT.Square,
-                )
-                if g % S_QUANT_PASSES == S_QUANT_PASSES - 1:
-                    kept = slice((g + 1 - S_QUANT_PASSES) * TOKENS, (g + 1) * TOKENS)
-                    nc.vector.quantize_mx(
-                        out=xs_codes[:, kept].bitcast(FP8X4), scales=xs_scales[:, kept],
-                        in_=xs_grouped[:],
-                    )
-                    nc.vector.quantize_mx(
-                        out=ss_codes[:, kept].bitcast(FP8X4), scales=ss_scales[:, kept],
-                        in_=ss_grouped[:],
-                    )
+            for i in range(W_EARLY + 2):
+                if i % MW_LOAD == 0 and i + MW_LOAD < PASSES:
+                    load_mod_w(i // MW_LOAD + 1)
+                if i % W_LOAD == 0 and i <= PASSES:
+                    load_weight(i // W_LOAD)
+                if i % X_LOAD == 2 and i + 2 < PASSES:
+                    load_x((i + 2) // X_LOAD)
+                if i < PASSES:
+                    turn_mod_w(i)
+                if i >= 2:
+                    turn_weight(i - 2)
+                if 1 <= i <= PASSES:
+                    quantise_mod_w(i - 1)
+                if 4 <= i < PASSES + 3 and i % PAIR == 0:
+                    quantise_products((i - 4) // PAIR)
+                if 2 <= i < PASSES + 2:
+                    products(i - 2)
+                if 1 <= i <= PASSES:
+                    first_matmul(i - 1)
 
         with ExitStack() as stage2:
             w_work = stage2.enter_context(tc.tile_pool(name="w_work", bufs=3, reuse_waits="tile"))
             tail = stage2.enter_context(tc.tile_pool(name="tail", bufs=2, reuse_waits="tile"))
-            w_turned = stage2.enter_context(tc.psum_pool(name="w_turned", bufs=4, reuse_waits="tile"))
             sums = stage2.enter_context(tc.psum_pool(name="sums", bufs=1, reuse_waits="tile"))
 
-            for h in range(HALVES):
-                y_sums = []
-                q_sums = []
-                for a in range(TOKEN_TILES):
-                    y_bank = sums.tile([P, BANK], F32, name="y_bank%d" % a)
-                    q_bank = sums.tile([P, BANK], F32, name="q_bank%d" % a)
-                    y_sums.append(y_bank)
-                    q_sums.append(q_bank)
+            w_squared = {}
+            w_codes = {}
+            w_scales = {}
+            w2_codes = {}
+            w2_scales = {}
+            y_sums = {}
+            q_sums = {}
 
-                for g0 in range(0, PASSES, W_BATCH_PASSES):
-                    if g0 % W_LOAD_PASSES == 0:
-                        w_raw = w_in.tile([P, ROW_TILES, W_LOAD_PASSES * K_PASS], BF16)
-                        nc.sync.dma_start(
-                            out=w_raw[:],
-                            in_=weight_rows[:, h, :, g0 * K_PASS : (g0 + W_LOAD_PASSES) * K_PASS],
+            def square(pair):
+                squared = w_work.tile([P, PAIR_COLS], BF16, align_bytes=64, name="w_squared")
+                nc.vector.tensor_tensor(
+                    out=squared[:, :SQUARE_COLS_VECTOR],
+                    in0=w_grouped[pair][:, :SQUARE_COLS_VECTOR],
+                    in1=w_grouped[pair][:, :SQUARE_COLS_VECTOR],
+                    op=ALU.mult,
+                )
+                nc.scalar.activation(
+                    out=squared[:, SQUARE_COLS_VECTOR:],
+                    in_=w_grouped[pair][:, SQUARE_COLS_VECTOR:],
+                    func=ACT.Square,
+                )
+                w_squared[pair] = squared
+
+            def quantise(pair):
+                codes = w_work.tile([P, PAIR_COLS // 4], U32, align_bytes=64, name="w_codes")
+                scales = w_work.tile([P, PAIR_COLS // 4], U8, align_bytes=64, name="w_scales")
+                nc.vector.quantize_mx(
+                    out=codes[:].bitcast(FP8X4), scales=scales[:], in_=w_grouped[pair][:]
+                )
+                codes2 = w_work.tile([P, PAIR_COLS // 4], U32, align_bytes=64, name="w2_codes")
+                scales2 = w_work.tile([P, PAIR_COLS // 4], U8, align_bytes=64, name="w2_scales")
+                nc.vector.quantize_mx(
+                    out=codes2[:].bitcast(FP8X4), scales=scales2[:], in_=w_squared[pair][:]
+                )
+                w_codes[pair] = codes
+                w_scales[pair] = scales
+                w2_codes[pair] = codes2
+                w2_scales[pair] = scales2
+
+            def multiply_into(banks, still_codes, still_scales, moving_codes, moving_scales, pair):
+                for gl in range(PAIR):
+                    g = (pair * PAIR + gl) % PASSES
+                    moving = slice(gl * ROUND_OUT, (gl + 1) * ROUND_OUT)
+                    for a in range(TOKEN_TILES):
+                        still = slice(g * TOKENS + a * P, g * TOKENS + (a + 1) * P)
+                        nc.tensor.matmul_mx(
+                            out=banks[a][:],
+                            lhsT=still_codes[:, still].bitcast(FP8X4),
+                            lhsT_scale=still_scales[:, still],
+                            rhs=moving_codes[:, moving].bitcast(FP8X4),
+                            rhs_scale=moving_scales[:, moving],
+                            start=(g == 0),
+                            stop=(g == PASSES - 1),
                         )
 
-                    w_grouped = w_work.tile([P, W_BATCH_COLS], BF16, align_bytes=64)
-                    w_words = w_grouped[:].bitcast(F32).rearrange(
-                        "p (g n o u) -> p g n o u", g=W_BATCH_PASSES, n=2, u=2
-                    )
-                    for gl in range(W_BATCH_PASSES):
-                        for n in range(2):
-                            w_bank = w_turned.tile([P, BANK], F32)
-                            for u in range(2):
-                                for b in range(2):
-                                    transpose_words(
-                                        nc, w_bank[:, (2 * u + b) * P : (2 * u + b + 1) * P],
-                                        w_raw[:, 2 * n + b, :],
-                                        ((g0 + gl) % W_LOAD_PASSES) * WORDS + u * P, ident[:],
-                                    )
-                            nc.scalar.copy(
-                                out=w_words[:, gl, n],
-                                in_=w_bank[:].rearrange("p (u o) -> p o u", u=2),
-                            )
-                    w_squared = w_work.tile([P, W_BATCH_COLS], BF16, align_bytes=64)
-                    nc.vector.tensor_tensor(
-                        out=w_squared[:, :SQUARE_COLS_VECTOR],
-                        in0=w_grouped[:, :SQUARE_COLS_VECTOR],
-                        in1=w_grouped[:, :SQUARE_COLS_VECTOR],
-                        op=ALU.mult,
-                    )
-                    nc.scalar.activation(
-                        out=w_squared[:, SQUARE_COLS_VECTOR:],
-                        in_=w_grouped[:, SQUARE_COLS_VECTOR:],
-                        func=ACT.Square,
-                    )
-                    w_codes = w_work.tile([P, W_BATCH_COLS // 4], U32, align_bytes=64)
-                    w_scales = w_work.tile([P, W_BATCH_COLS // 4], U8, align_bytes=64)
-                    nc.vector.quantize_mx(
-                        out=w_codes[:].bitcast(FP8X4), scales=w_scales[:], in_=w_grouped[:]
-                    )
-                    w2_codes = w_work.tile([P, W_BATCH_COLS // 4], U32, align_bytes=64)
-                    w2_scales = w_work.tile([P, W_BATCH_COLS // 4], U8, align_bytes=64)
-                    nc.vector.quantize_mx(
-                        out=w2_codes[:].bitcast(FP8X4), scales=w2_scales[:], in_=w_squared[:]
-                    )
+            def multiply(pair):
+                if pair % ROUND_PAIRS == 0:
+                    for a in range(TOKEN_TILES):
+                        y_bank = sums.tile([P, BANK], F32, name="y_bank%d" % a)
+                        q_bank = sums.tile([P, BANK], F32, name="q_bank%d" % a)
+                        y_sums[a] = y_bank
+                        q_sums[a] = q_bank
+                multiply_into(q_sums, ss_codes, ss_scales, w2_codes[pair], w2_scales[pair], pair)
+                multiply_into(y_sums, xs_codes, xs_scales, w_codes[pair], w_scales[pair], pair)
 
-                    for gl in range(W_BATCH_PASSES):
-                        g = g0 + gl
-                        moving = slice(gl * OUT_HALF, (gl + 1) * OUT_HALF)
-                        for a in range(TOKEN_TILES):
-                            still = slice(g * TOKENS + a * P, g * TOKENS + (a + 1) * P)
-                            nc.tensor.matmul_mx(
-                                out=q_sums[a][:],
-                                lhsT=ss_codes[:, still].bitcast(FP8X4),
-                                lhsT_scale=ss_scales[:, still],
-                                rhs=w2_codes[:, moving].bitcast(FP8X4),
-                                rhs_scale=w2_scales[:, moving],
-                                start=(g == 0),
-                                stop=(g == PASSES - 1),
-                            )
-                        for a in range(TOKEN_TILES):
-                            still = slice(g * TOKENS + a * P, g * TOKENS + (a + 1) * P)
-                            nc.tensor.matmul_mx(
-                                out=y_sums[a][:],
-                                lhsT=xs_codes[:, still].bitcast(FP8X4),
-                                lhsT_scale=xs_scales[:, still],
-                                rhs=w_codes[:, moving].bitcast(FP8X4),
-                                rhs_scale=w_scales[:, moving],
-                                start=(g == 0),
-                                stop=(g == PASSES - 1),
-                            )
-
+            def finish_round(h):
+                results = []
                 for a in range(TOKEN_TILES):
-                    demod = tail.tile([P, OUT_HALF], F32)
+                    demod = tail.tile([P, ROUND_OUT], F32)
                     nc.scalar.activation(
                         out=demod[:], in_=q_sums[a][:], func=ACT.Abs_reciprocal_sqrt, bias=eps[:]
                     )
-                    result = tail.tile([P, OUT_HALF], F32)
+                    result = tail.tile([P, ROUND_OUT], F32)
+                    nc.vector.tensor_tensor(out=result[:], in0=y_sums[a][:], in1=demod[:], op=ALU.mult)
+                    results.append(result)
+                for a in range(TOKEN_TILES):
                     nc.vector.tensor_tensor(
-                        out=result[:], in0=y_sums[a][:], in1=demod[:], op=ALU.mult
-                    )
-                    nc.vector.tensor_tensor(
-                        out=result[:], in0=result[:],
-                        in1=bias_all[:, h * OUT_HALF : (h + 1) * OUT_HALF], op=ALU.add,
+                        out=results[a][:], in0=results[a][:],
+                        in1=bias_all[:, h * ROUND_OUT : (h + 1) * ROUND_OUT], op=ALU.add,
                     )
                     nc.sync.dma_start(
-                        out=out_rows[a * P : (a + 1) * P, h * OUT_HALF : (h + 1) * OUT_HALF],
-                        in_=result[:],
+                        out=out_rows[a * P : (a + 1) * P, h * ROUND_OUT : (h + 1) * ROUND_OUT],
+                        in_=results[a][:],
                     )
+
+            square(0)
+            for b in range(W_PAIRS + 1):
+                if b % W_LOAD == 0 and PASSES // W_LOAD + 1 + b // W_LOAD < W_PASSES // W_LOAD:
+                    load_weight(PASSES // W_LOAD + 1 + b // W_LOAD)
+                if b == ROUND_PAIRS + 1:
+                    finish_round(0)
+                if b + 1 < W_PAIRS:
+                    square(b + 1)
+                if b < W_PAIRS:
+                    quantise(b)
+                if W_EARLY + b < W_PASSES:
+                    turn_weight(W_EARLY + b)
+                if b >= 1:
+                    multiply(b - 1)
+            finish_round(1)

@@ -28,14 +28,16 @@ ROUNDS = OUT_DIM // ROUND_OUT
 ROW_TILES = ROUND_OUT // P
 W_PASSES = ROUNDS * PASSES
 
-MW_LOAD = 2
-X_LOAD = 4
-W_LOAD = 4
+X_LOAD = 2
+W_LOAD = 2
+AHEAD = 3
 PAIR = 2
 PAIR_COLS = PAIR * ROUND_OUT * 4
 W_PAIRS = W_PASSES // PAIR
 ROUND_PAIRS = PASSES // PAIR
-W_EARLY = PASSES + 2
+STAGE1_TURNS = PASSES + 4
+W_LAG = 2
+W_EARLY = STAGE1_TURNS - W_LAG
 KEPT_PAIRS = W_EARLY // PAIR
 
 SQUARE_COLS_VECTOR = 1920
@@ -60,7 +62,7 @@ def tile_modulatedlinear_k_kernel(tc, x, modulation, weight, bias, mod_w, mod_b,
     with ExitStack() as whole:
         whole.enter_context(tc.manual_schedule())
         const = whole.enter_context(tc.tile_pool(name="const", bufs=1))
-        w_in = whole.enter_context(tc.tile_pool(name="w_in", bufs=2))
+        w_in = whole.enter_context(tc.tile_pool(name="w_in", bufs=3))
         w_kept = whole.enter_context(tc.tile_pool(name="w_kept", bufs=KEPT_PAIRS))
         w_turned = whole.enter_context(tc.psum_pool(name="w_turned", bufs=2))
 
@@ -95,6 +97,10 @@ def tile_modulatedlinear_k_kernel(tc, x, modulation, weight, bias, mod_w, mod_b,
             )
             w_raw[load] = raw
 
+        def issue_weight_load(turn):
+            if (turn - W_LAG) % W_LOAD == 0 and 0 <= turn - W_LAG < W_PASSES:
+                load_weight((turn - W_LAG) // W_LOAD)
+
         def turn_weight(w):
             if w % PAIR == 0:
                 grouped = w_kept.tile([P, PAIR_COLS], BF16, align_bytes=64, name="w_grouped")
@@ -117,14 +123,15 @@ def tile_modulatedlinear_k_kernel(tc, x, modulation, weight, bias, mod_w, mod_b,
 
         with ExitStack() as stage1:
             once = stage1.enter_context(tc.tile_pool(name="once", bufs=1))
-            loads = stage1.enter_context(tc.tile_pool(name="loads", bufs=2))
-            work = stage1.enter_context(tc.tile_pool(name="work", bufs=2))
+            mw_in = stage1.enter_context(tc.tile_pool(name="mw_in", bufs=AHEAD + 1))
+            x_in = stage1.enter_context(tc.tile_pool(name="x_in", bufs=3))
+            work = stage1.enter_context(tc.tile_pool(name="work", bufs=3))
             turned = stage1.enter_context(tc.psum_pool(name="turned", bufs=2))
             turned_x = stage1.enter_context(tc.psum_pool(name="turned_x", bufs=2))
             s_psum = stage1.enter_context(tc.psum_pool(name="s_psum", bufs=2))
 
-            mw_raw = {}
             x_raw = {}
+            mw_raw = {}
             mw_grouped = {}
             mw_codes = {}
             mw_scales = {}
@@ -133,21 +140,25 @@ def tile_modulatedlinear_k_kernel(tc, x, modulation, weight, bias, mod_w, mod_b,
             xs_grouped = {}
             ss_grouped = {}
 
-            def load_mod_w(load):
-                raw = loads.tile([P, 2 * MW_LOAD, 2, MOD_DIM], BF16, name="mw_raw")
-                nc.sync.dma_start(
-                    out=raw[:],
-                    in_=mod_w_rows[:, 2 * MW_LOAD * load : 2 * MW_LOAD * (load + 1), :, :],
-                )
-                mw_raw[load] = raw
+            def load_mod_w(g):
+                raw = mw_in.tile([P, 2, 2, MOD_DIM], BF16, name="mw_raw")
+                nc.sync.dma_start(out=raw[:], in_=mod_w_rows[:, 2 * g : 2 * (g + 1), :, :])
+                mw_raw[g] = raw
 
             def load_x(load):
-                raw = loads.tile([P, TOKEN_TILES, X_LOAD * K_PASS], BF16, name="x_raw")
+                raw = x_in.tile([P, TOKEN_TILES, X_LOAD * K_PASS], BF16, name="x_raw")
                 nc.sync.dma_start(
                     out=raw[:],
                     in_=x_rows[:, :, load * X_LOAD * K_PASS : (load + 1) * X_LOAD * K_PASS],
                 )
                 x_raw[load] = raw
+
+            def issue_loads(turn):
+                if turn < PASSES:
+                    load_mod_w(turn)
+                if (turn - 1) % X_LOAD == 0 and turn - 1 < PASSES:
+                    load_x((turn - 1) // X_LOAD)
+                issue_weight_load(turn)
 
             def turn_mod_w(g):
                 grouped = work.tile([P, 4 * P * 4], BF16, align_bytes=64, name="mw_grouped")
@@ -158,7 +169,7 @@ def tile_modulatedlinear_k_kernel(tc, x, modulation, weight, bias, mod_w, mod_b,
                         for v in range(2):
                             transpose_words(
                                 nc, mw_bank[:, (2 * e + v) * P : (2 * e + v + 1) * P],
-                                mw_raw[g // MW_LOAD][:, 2 * (g % MW_LOAD) + u, e, :], v * P, ident[:],
+                                mw_raw[g][:, u, e, :], v * P, ident[:],
                             )
                     nc.scalar.copy(
                         out=words[:, u], in_=mw_bank[:].rearrange("p (e v r) -> p e r v", e=2, v=2)
@@ -211,45 +222,41 @@ def tile_modulatedlinear_k_kernel(tc, x, modulation, weight, bias, mod_w, mod_b,
                 s_values[g] = s_sb
 
             def products(g):
-                if g % PAIR == 0:
-                    xs_pair = work.tile([P, PAIR * TOKENS * 4], BF16, align_bytes=64, name="xs_grouped")
-                    ss_pair = work.tile([P, PAIR * TOKENS * 4], BF16, align_bytes=64, name="ss_grouped")
-                    xs_grouped[g // PAIR] = xs_pair
-                    ss_grouped[g // PAIR] = ss_pair
-                cols = slice((g % PAIR) * TOKENS * 4, (g % PAIR + 1) * TOKENS * 4)
+                xs = work.tile([P, TOKENS * 4], BF16, align_bytes=64, name="xs_grouped")
+                ss = work.tile([P, TOKENS * 4], BF16, align_bytes=64, name="ss_grouped")
                 s_view = s_values[g][:].rearrange("p (u t e) -> p t u e", u=2, e=2)
                 nc.vector.tensor_tensor(
-                    out=xs_grouped[g // PAIR][:, cols].rearrange("p (t u e) -> p t u e", u=2, e=2),
+                    out=xs[:].rearrange("p (t u e) -> p t u e", u=2, e=2),
                     in0=x_banks[g][:].bitcast(BF16).rearrange("p (u t e) -> p t u e", u=2, e=2),
                     in1=s_view,
                     op=ALU.mult,
                 )
                 nc.scalar.activation(
-                    out=ss_grouped[g // PAIR][:, cols].rearrange("p (t u e) -> p t u e", u=2, e=2),
-                    in_=s_view,
-                    func=ACT.Square,
+                    out=ss[:].rearrange("p (t u e) -> p t u e", u=2, e=2), in_=s_view, func=ACT.Square
                 )
+                xs_grouped[g] = xs
+                ss_grouped[g] = ss
 
-            def quantise_products(pair):
-                kept = slice(pair * PAIR * TOKENS, (pair + 1) * PAIR * TOKENS)
+            def quantise_products(g):
+                kept = slice(g * TOKENS, (g + 1) * TOKENS)
                 nc.vector.quantize_mx(
                     out=xs_codes[:, kept].bitcast(FP8X4), scales=xs_scales[:, kept],
-                    in_=xs_grouped[pair][:],
+                    in_=xs_grouped[g][:],
                 )
                 nc.vector.quantize_mx(
                     out=ss_codes[:, kept].bitcast(FP8X4), scales=ss_scales[:, kept],
-                    in_=ss_grouped[pair][:],
+                    in_=ss_grouped[g][:],
                 )
 
             mod_raw = once.tile([P, TOKEN_TILES, MOD_DIM], BF16)
             nc.sync.dma_start(out=mod_raw[:], in_=modulation_rows)
-            load_mod_w(0)
             mod_b_raw = once.tile([P, 2 * P], BF16)
             nc.vector.memset(mod_b_raw[:], 0.0)
             nc.sync.dma_start(
                 out=mod_b_raw[: 2 * PASSES, :], in_=mod_b.rearrange("(c w) -> c w", w=2 * P)
             )
-            load_x(0)
+            for t in range(AHEAD):
+                issue_loads(t)
 
             mod_bank = turned.tile([P, BANK], F32, tag="bank")
             for u in range(2):
@@ -273,21 +280,16 @@ def tile_modulatedlinear_k_kernel(tc, x, modulation, weight, bias, mod_w, mod_b,
             transpose_words(nc, mod_b_bank[:, :P], mod_b_raw[:], 0, ident[:])
             nc.vector.tensor_copy(out=mod_b_cols[:], in_=mod_b_bank[:, : 2 * PASSES].bitcast(BF16))
 
-            for i in range(W_EARLY + 2):
-                if i % MW_LOAD == 0 and i + MW_LOAD < PASSES:
-                    load_mod_w(i // MW_LOAD + 1)
-                if i % W_LOAD == 0 and i <= PASSES:
-                    load_weight(i // W_LOAD)
-                if i % X_LOAD == 2 and i + 2 < PASSES:
-                    load_x((i + 2) // X_LOAD)
+            for i in range(STAGE1_TURNS):
+                issue_loads(i + AHEAD)
                 if i < PASSES:
                     turn_mod_w(i)
-                if i >= 2:
-                    turn_weight(i - 2)
+                if i >= W_LAG:
+                    turn_weight(i - W_LAG)
                 if 1 <= i <= PASSES:
                     quantise_mod_w(i - 1)
-                if 4 <= i < PASSES + 3 and i % PAIR == 0:
-                    quantise_products((i - 4) // PAIR)
+                if 3 <= i < PASSES + 3:
+                    quantise_products(i - 3)
                 if 2 <= i < PASSES + 2:
                     products(i - 2)
                 if 1 <= i <= PASSES:
@@ -385,8 +387,7 @@ def tile_modulatedlinear_k_kernel(tc, x, modulation, weight, bias, mod_w, mod_b,
 
             square(0)
             for b in range(W_PAIRS + 1):
-                if b % W_LOAD == 0 and PASSES // W_LOAD + 1 + b // W_LOAD < W_PASSES // W_LOAD:
-                    load_weight(PASSES // W_LOAD + 1 + b // W_LOAD)
+                issue_weight_load(STAGE1_TURNS + b + AHEAD)
                 if b == ROUND_PAIRS + 1:
                     finish_round(0)
                 if b + 1 < W_PAIRS:

@@ -76,10 +76,8 @@ def tile_modulatedlinear_k_kernel(tc, x, modulation, weight, bias, mod_w, mod_b,
         bias_all = const.tile([P, OUT_DIM], BF16)
         nc.gpsimd.dma_start(out=bias_all[:], in_=bias.partition_broadcast(P))
 
-        xs_codes = const.tile([P, PASSES * TOKENS], U32, align_bytes=64)
-        xs_scales = const.tile([P, PASSES * TOKENS], U8, align_bytes=64)
-        ss_codes = const.tile([P, PASSES * TOKENS], U32, align_bytes=64)
-        ss_scales = const.tile([P, PASSES * TOKENS], U8, align_bytes=64)
+        prod_codes = const.tile([P, PASSES * 2 * TOKENS], U32, align_bytes=64)
+        prod_scales = const.tile([P, PASSES * 2 * TOKENS], U8, align_bytes=64)
         mod_b_cols = const.tile([P, 4 * PASSES], F32)
 
         w_raw = {}
@@ -137,8 +135,7 @@ def tile_modulatedlinear_k_kernel(tc, x, modulation, weight, bias, mod_w, mod_b,
             mw_scales = {}
             x_banks = {}
             s_values = {}
-            xs_grouped = {}
-            ss_grouped = {}
+            prod_grouped = {}
 
             def load_mod_w(g):
                 raw = mw_in.tile([P, 2, 2, MOD_DIM], BF16, name="mw_raw")
@@ -222,30 +219,26 @@ def tile_modulatedlinear_k_kernel(tc, x, modulation, weight, bias, mod_w, mod_b,
                 s_values[g] = s_sb
 
             def products(g):
-                xs = work.tile([P, TOKENS * 4], BF16, align_bytes=64, name="xs_grouped")
-                ss = work.tile([P, TOKENS * 4], BF16, align_bytes=64, name="ss_grouped")
+                prod = work.tile([P, 2 * TOKENS * 4], BF16, align_bytes=64, name="prod_grouped")
                 s_view = s_values[g][:].rearrange("p (u t e) -> p t u e", u=2, e=2)
                 nc.vector.tensor_tensor(
-                    out=xs[:].rearrange("p (t u e) -> p t u e", u=2, e=2),
+                    out=prod[:, : TOKENS * 4].rearrange("p (t u e) -> p t u e", u=2, e=2),
                     in0=x_banks[g][:].bitcast(BF16).rearrange("p (u t e) -> p t u e", u=2, e=2),
                     in1=s_view,
                     op=ALU.mult,
                 )
                 nc.scalar.activation(
-                    out=ss[:].rearrange("p (t u e) -> p t u e", u=2, e=2), in_=s_view, func=ACT.Square
+                    out=prod[:, TOKENS * 4 :].rearrange("p (t u e) -> p t u e", u=2, e=2),
+                    in_=s_view,
+                    func=ACT.Square,
                 )
-                xs_grouped[g] = xs
-                ss_grouped[g] = ss
+                prod_grouped[g] = prod
 
             def quantise_products(g):
-                kept = slice(g * TOKENS, (g + 1) * TOKENS)
+                kept = slice(g * 2 * TOKENS, (g + 1) * 2 * TOKENS)
                 nc.vector.quantize_mx(
-                    out=xs_codes[:, kept].bitcast(FP8X4), scales=xs_scales[:, kept],
-                    in_=xs_grouped[g][:],
-                )
-                nc.vector.quantize_mx(
-                    out=ss_codes[:, kept].bitcast(FP8X4), scales=ss_scales[:, kept],
-                    in_=ss_grouped[g][:],
+                    out=prod_codes[:, kept].bitcast(FP8X4), scales=prod_scales[:, kept],
+                    in_=prod_grouped[g][:],
                 )
 
             mod_raw = once.tile([P, TOKEN_TILES, MOD_DIM], BF16)
@@ -324,31 +317,31 @@ def tile_modulatedlinear_k_kernel(tc, x, modulation, weight, bias, mod_w, mod_b,
                 w_squared[pair] = squared
 
             def quantise(pair):
-                codes = w_work.tile([P, PAIR_COLS // 4], U32, align_bytes=64, name="w_codes")
-                scales = w_work.tile([P, PAIR_COLS // 4], U8, align_bytes=64, name="w_scales")
-                nc.vector.quantize_mx(
-                    out=codes[:].bitcast(FP8X4), scales=scales[:], in_=w_grouped[pair][:]
-                )
                 codes2 = w_work.tile([P, PAIR_COLS // 4], U32, align_bytes=64, name="w2_codes")
                 scales2 = w_work.tile([P, PAIR_COLS // 4], U8, align_bytes=64, name="w2_scales")
                 nc.vector.quantize_mx(
                     out=codes2[:].bitcast(FP8X4), scales=scales2[:], in_=w_squared[pair][:]
+                )
+                codes = w_work.tile([P, PAIR_COLS // 4], U32, align_bytes=64, name="w_codes")
+                scales = w_work.tile([P, PAIR_COLS // 4], U8, align_bytes=64, name="w_scales")
+                nc.vector.quantize_mx(
+                    out=codes[:].bitcast(FP8X4), scales=scales[:], in_=w_grouped[pair][:]
                 )
                 w_codes[pair] = codes
                 w_scales[pair] = scales
                 w2_codes[pair] = codes2
                 w2_scales[pair] = scales2
 
-            def multiply_into(banks, still_codes, still_scales, moving_codes, moving_scales, pair):
+            def multiply_into(banks, product, moving_codes, moving_scales, pair):
                 for gl in range(PAIR):
                     g = (pair * PAIR + gl) % PASSES
                     moving = slice(gl * ROUND_OUT, (gl + 1) * ROUND_OUT)
                     for a in range(TOKEN_TILES):
-                        still = slice(g * TOKENS + a * P, g * TOKENS + (a + 1) * P)
+                        first = (2 * g + product) * TOKENS + a * P
                         nc.tensor.matmul_mx(
                             out=banks[a][:],
-                            lhsT=still_codes[:, still].bitcast(FP8X4),
-                            lhsT_scale=still_scales[:, still],
+                            lhsT=prod_codes[:, first : first + P].bitcast(FP8X4),
+                            lhsT_scale=prod_scales[:, first : first + P],
                             rhs=moving_codes[:, moving].bitcast(FP8X4),
                             rhs_scale=moving_scales[:, moving],
                             start=(g == 0),
@@ -359,11 +352,11 @@ def tile_modulatedlinear_k_kernel(tc, x, modulation, weight, bias, mod_w, mod_b,
                 if pair % ROUND_PAIRS == 0:
                     for a in range(TOKEN_TILES):
                         y_bank = sums.tile([P, BANK], F32, name="y_bank%d" % a)
-                        q_bank = sums.tile([P, BANK], F32, name="q_bank%d" % a)
+                        q_bank = sums.tile([P, BANK], F32, name="q_bank%d" % a, bufs=2)
                         y_sums[a] = y_bank
                         q_sums[a] = q_bank
-                multiply_into(q_sums, ss_codes, ss_scales, w2_codes[pair], w2_scales[pair], pair)
-                multiply_into(y_sums, xs_codes, xs_scales, w_codes[pair], w_scales[pair], pair)
+                multiply_into(q_sums, 1, w2_codes[pair], w2_scales[pair], pair)
+                multiply_into(y_sums, 0, w_codes[pair], w_scales[pair], pair)
 
             def finish_round(h):
                 results = []

@@ -40,7 +40,7 @@ W_LAG = 2
 W_EARLY = STAGE1_TURNS - W_LAG
 KEPT_PAIRS = W_EARLY // PAIR
 
-SQUARE_COLS_VECTOR = 1920
+SQUARE_COLS_VECTOR = 2176
 
 FLOPS = 2 * TOKENS * (MOD_DIM * IN_DIM + 2 * IN_DIM * OUT_DIM)
 

from contextlib import ExitStack

import concourse.mybir as mybir
from concourse.masks import make_identity

F32 = mybir.dt.float32
BF16 = mybir.dt.bfloat16
U32 = mybir.dt.uint32
U8 = mybir.dt.uint8
FP8X4 = mybir.dt.float8_e4m3fn_x4
ACT = mybir.ActivationFunctionType
ALU = mybir.AluOpType

P = 128
TOKENS = 256
IN_DIM = 8192
OUT_DIM = 1024
MOD_DIM = 512
EPS = 1e-8

K_PASS = 512
PASSES = IN_DIM // K_PASS
WORDS = K_PASS // 2
BANK = 512
TOKEN_TILES = TOKENS // P
ROUND_OUT = 512
ROUNDS = OUT_DIM // ROUND_OUT
ROW_TILES = ROUND_OUT // P
W_PASSES = ROUNDS * PASSES

X_LOAD = 2
W_LOAD = 2
AHEAD = 3
PAIR = 2
PAIR_COLS = PAIR * ROUND_OUT * 4
W_PAIRS = W_PASSES // PAIR
ROUND_PAIRS = PASSES // PAIR
STAGE1_TURNS = PASSES + 4
W_LAG = 2
W_EARLY = STAGE1_TURNS - W_LAG
KEPT_PAIRS = W_EARLY // PAIR

SQUARE_COLS_VECTOR = 2176

FLOPS = 2 * TOKENS * (MOD_DIM * IN_DIM + 2 * IN_DIM * OUT_DIM)


def transpose_words(nc, bank_cols, rows_bf16, first_word, ident):
    nc.tensor.transpose(
        bank_cols, rows_bf16.bitcast(F32)[:, first_word : first_word + P], ident
    )


def tile_modulatedlinear_k_kernel(tc, x, modulation, weight, bias, mod_w, mod_b, out):
    nc = tc.nc
    x_rows = x.flatten_outer_dims().rearrange("(a r) i -> r a i", r=P)
    modulation_rows = modulation.flatten_outer_dims().rearrange("(a r) k -> r a k", r=P)
    out_rows = out.flatten_outer_dims()
    mod_w_rows = mod_w.rearrange("(c r e) k -> r c e k", r=P, e=2)
    weight_rows = weight.rearrange("(h b r) i -> r h b i", b=ROW_TILES, r=P)

    with ExitStack() as whole:
        whole.enter_context(tc.manual_schedule())
        const = whole.enter_context(tc.tile_pool(name="const", bufs=1))
        w_in = whole.enter_context(tc.tile_pool(name="w_in", bufs=3))
        w_kept = whole.enter_context(tc.tile_pool(name="w_kept", bufs=KEPT_PAIRS))
        w_turned = whole.enter_context(tc.psum_pool(name="w_turned", bufs=2))

        ident = const.tile([P, P], F32)
        make_identity(nc, ident[:])
        eps = const.tile([P, 1], F32)
        nc.vector.memset(eps[:], EPS)
        table_warm = const.tile([P, 1], F32)
        nc.scalar.activation(out=table_warm[:], in_=eps[:], func=ACT.Abs_reciprocal_sqrt)

        bias_all = const.tile([P, OUT_DIM], BF16)
        nc.gpsimd.dma_start(out=bias_all[:], in_=bias.partition_broadcast(P))

        prod_codes = const.tile([P, PASSES * 2 * TOKENS], U32, align_bytes=64)
        prod_scales = const.tile([P, PASSES * 2 * TOKENS], U8, align_bytes=64)
        mod_b_cols = const.tile([P, 4 * PASSES], F32)

        w_raw = {}
        w_grouped = {}

        def load_weight(load):
            first = load * W_LOAD
            raw = w_in.tile([P, ROW_TILES, W_LOAD * K_PASS], BF16, name="w_raw")
            nc.sync.dma_start(
                out=raw[:],
                in_=weight_rows[
                    :, first // PASSES, :,
                    (first % PASSES) * K_PASS : (first % PASSES + W_LOAD) * K_PASS,
                ],
            )
            w_raw[load] = raw

        def issue_weight_load(turn):
            if (turn - W_LAG) % W_LOAD == 0 and 0 <= turn - W_LAG < W_PASSES:
                load_weight((turn - W_LAG) // W_LOAD)

        def turn_weight(w):
            if w % PAIR == 0:
                grouped = w_kept.tile([P, PAIR_COLS], BF16, align_bytes=64, name="w_grouped")
                w_grouped[w // PAIR] = grouped
            words = w_grouped[w // PAIR][:].bitcast(F32).rearrange(
                "p (g n o u) -> p g n o u", g=PAIR, n=2, u=2
            )
            for n in range(2):
                w_bank = w_turned.tile([P, BANK], F32)
                for u in range(2):
                    for b in range(2):
                        transpose_words(
                            nc, w_bank[:, (2 * u + b) * P : (2 * u + b + 1) * P],
                            w_raw[w // W_LOAD][:, 2 * n + b, :],
                            (w % W_LOAD) * WORDS + u * P, ident[:],
                        )
                nc.scalar.copy(
                    out=words[:, w % PAIR, n], in_=w_bank[:].rearrange("p (u o) -> p o u", u=2)
                )

        with ExitStack() as stage1:
            once = stage1.enter_context(tc.tile_pool(name="once", bufs=1))
            mw_in = stage1.enter_context(tc.tile_pool(name="mw_in", bufs=AHEAD + 1))
            x_in = stage1.enter_context(tc.tile_pool(name="x_in", bufs=3))
            work = stage1.enter_context(tc.tile_pool(name="work", bufs=3))
            turned = stage1.enter_context(tc.psum_pool(name="turned", bufs=2))
            turned_x = stage1.enter_context(tc.psum_pool(name="turned_x", bufs=2))
            s_psum = stage1.enter_context(tc.psum_pool(name="s_psum", bufs=2))

            x_raw = {}
            mw_raw = {}
            mw_grouped = {}
            mw_codes = {}
            mw_scales = {}
            x_banks = {}
            s_values = {}
            prod_grouped = {}

            def load_mod_w(g):
                raw = mw_in.tile([P, 2, 2, MOD_DIM], BF16, name="mw_raw")
                nc.sync.dma_start(out=raw[:], in_=mod_w_rows[:, 2 * g : 2 * (g + 1), :, :])
                mw_raw[g] = raw

            def load_x(load):
                raw = x_in.tile([P, TOKEN_TILES, X_LOAD * K_PASS], BF16, name="x_raw")
                nc.sync.dma_start(
                    out=raw[:],
                    in_=x_rows[:, :, load * X_LOAD * K_PASS : (load + 1) * X_LOAD * K_PASS],
                )
                x_raw[load] = raw

            def issue_loads(turn):
                if turn < PASSES:
                    load_mod_w(turn)
                if (turn - 1) % X_LOAD == 0 and turn - 1 < PASSES:
                    load_x((turn - 1) // X_LOAD)
                issue_weight_load(turn)

            def turn_mod_w(g):
                grouped = work.tile([P, 4 * P * 4], BF16, align_bytes=64, name="mw_grouped")
                words = grouped[:].bitcast(F32).rearrange("p (u e r v) -> p u e r v", u=2, e=2, v=2)
                for u in range(2):
                    mw_bank = turned.tile([P, BANK], F32, tag="bank")
                    for e in range(2):
                        for v in range(2):
                            transpose_words(
                                nc, mw_bank[:, (2 * e + v) * P : (2 * e + v + 1) * P],
                                mw_raw[g][:, u, e, :], v * P, ident[:],
                            )
                    nc.scalar.copy(
                        out=words[:, u], in_=mw_bank[:].rearrange("p (e v r) -> p e r v", e=2, v=2)
                    )
                mw_grouped[g] = grouped

            def quantise_mod_w(g):
                codes = work.tile([P, 4 * P], U32, align_bytes=64, name="mw_codes")
                scales = work.tile([P, 4 * P], U8, align_bytes=64, name="mw_scales")
                nc.vector.quantize_mx(
                    out=codes[:].bitcast(FP8X4), scales=scales[:], in_=mw_grouped[g][:]
                )
                mw_codes[g] = codes
                mw_scales[g] = scales

            def first_matmul(g):
                x_bank = turned_x.tile([P, BANK], F32)
                for u in range(2):
                    for a in range(TOKEN_TILES):
                        transpose_words(
                            nc, x_bank[:, (u * TOKEN_TILES + a) * P : (u * TOKEN_TILES + a + 1) * P],
                            x_raw[g // X_LOAD][:, a, :], (g % X_LOAD) * WORDS + u * P, ident[:],
                        )
                x_banks[g] = x_bank
                s_sb = work.tile([P, 4 * TOKENS], F32)
                s_halves = []
                for u in range(2):
                    s_bank = s_psum.tile([P, BANK], F32)
                    for e in range(2):
                        j = 2 * u + e
                        nc.tensor.matmul_mx(
                            out=s_bank[:, e * TOKENS : (e + 1) * TOKENS],
                            lhsT=mw_codes[g][:, j * P : (j + 1) * P].bitcast(FP8X4),
                            lhsT_scale=mw_scales[g][:, j * P : (j + 1) * P],
                            rhs=mod_codes[:].bitcast(FP8X4),
                            rhs_scale=mod_scales[:],
                            start=True,
                            stop=True,
                        )
                    s_halves.append(s_bank)
                for u in range(2):
                    nc.vector.tensor_tensor(
                        out=s_sb[:, u * BANK : (u + 1) * BANK].rearrange("p (t e) -> p t e", e=2),
                        in0=s_halves[u][:].rearrange("p (e t) -> p t e", e=2),
                        in1=mod_b_cols[:, 4 * g + 2 * u : 4 * g + 2 * u + 2]
                        .unsqueeze(1)
                        .to_broadcast([P, TOKENS, 2]),
                        op=ALU.add,
                    )
                s_values[g] = s_sb

            def products(g):
                prod = work.tile([P, 2 * TOKENS * 4], BF16, align_bytes=64, name="prod_grouped")
                s_view = s_values[g][:].rearrange("p (u t e) -> p t u e", u=2, e=2)
                nc.vector.tensor_tensor(
                    out=prod[:, : TOKENS * 4].rearrange("p (t u e) -> p t u e", u=2, e=2),
                    in0=x_banks[g][:].bitcast(BF16).rearrange("p (u t e) -> p t u e", u=2, e=2),
                    in1=s_view,
                    op=ALU.mult,
                )
                nc.scalar.activation(
                    out=prod[:, TOKENS * 4 :].rearrange("p (t u e) -> p t u e", u=2, e=2),
                    in_=s_view,
                    func=ACT.Square,
                )
                prod_grouped[g] = prod

            def quantise_products(g):
                kept = slice(g * 2 * TOKENS, (g + 1) * 2 * TOKENS)
                nc.vector.quantize_mx(
                    out=prod_codes[:, kept].bitcast(FP8X4), scales=prod_scales[:, kept],
                    in_=prod_grouped[g][:],
                )

            mod_raw = once.tile([P, TOKEN_TILES, MOD_DIM], BF16)
            nc.sync.dma_start(out=mod_raw[:], in_=modulation_rows)
            mod_b_raw = once.tile([P, 2 * P], BF16)
            nc.vector.memset(mod_b_raw[:], 0.0)
            nc.sync.dma_start(
                out=mod_b_raw[: 2 * PASSES, :], in_=mod_b.rearrange("(c w) -> c w", w=2 * P)
            )
            for t in range(AHEAD):
                issue_loads(t)

            mod_bank = turned.tile([P, BANK], F32, tag="bank")
            for u in range(2):
                for a in range(TOKEN_TILES):
                    transpose_words(
                        nc, mod_bank[:, (u * TOKEN_TILES + a) * P : (u * TOKEN_TILES + a + 1) * P],
                        mod_raw[:, a, :], u * P, ident[:],
                    )
            mod_grouped = once.tile([P, TOKENS * 4], BF16, align_bytes=64)
            nc.scalar.copy(
                out=mod_grouped[:].bitcast(F32).rearrange("p (t u) -> p t u", u=2),
                in_=mod_bank[:].rearrange("p (u t) -> p t u", u=2),
            )
            mod_codes = once.tile([P, TOKENS], U32, align_bytes=64)
            mod_scales = once.tile([P, TOKENS], U8, align_bytes=64)
            nc.vector.quantize_mx(
                out=mod_codes[:].bitcast(FP8X4), scales=mod_scales[:], in_=mod_grouped[:]
            )

            mod_b_bank = turned.tile([P, BANK], F32, tag="bank")
            transpose_words(nc, mod_b_bank[:, :P], mod_b_raw[:], 0, ident[:])
            nc.vector.tensor_copy(out=mod_b_cols[:], in_=mod_b_bank[:, : 2 * PASSES].bitcast(BF16))

            for i in range(STAGE1_TURNS):
                issue_loads(i + AHEAD)
                if i < PASSES:
                    turn_mod_w(i)
                if i >= W_LAG:
                    turn_weight(i - W_LAG)
                if 1 <= i <= PASSES:
                    quantise_mod_w(i - 1)
                if 3 <= i < PASSES + 3:
                    quantise_products(i - 3)
                if 2 <= i < PASSES + 2:
                    products(i - 2)
                if 1 <= i <= PASSES:
                    first_matmul(i - 1)

        with ExitStack() as stage2:
            w_work = stage2.enter_context(tc.tile_pool(name="w_work", bufs=3, reuse_waits="tile"))
            tail = stage2.enter_context(tc.tile_pool(name="tail", bufs=2, reuse_waits="tile"))
            sums = stage2.enter_context(tc.psum_pool(name="sums", bufs=1, reuse_waits="tile"))

            w_squared = {}
            w_codes = {}
            w_scales = {}
            w2_codes = {}
            w2_scales = {}
            y_sums = {}
            q_sums = {}

            def square(pair):
                squared = w_work.tile([P, PAIR_COLS], BF16, align_bytes=64, name="w_squared")
                nc.vector.tensor_tensor(
                    out=squared[:, :SQUARE_COLS_VECTOR],
                    in0=w_grouped[pair][:, :SQUARE_COLS_VECTOR],
                    in1=w_grouped[pair][:, :SQUARE_COLS_VECTOR],
                    op=ALU.mult,
                )
                nc.scalar.activation(
                    out=squared[:, SQUARE_COLS_VECTOR:],
                    in_=w_grouped[pair][:, SQUARE_COLS_VECTOR:],
                    func=ACT.Square,
                )
                w_squared[pair] = squared

            def quantise(pair):
                codes2 = w_work.tile([P, PAIR_COLS // 4], U32, align_bytes=64, name="w2_codes")
                scales2 = w_work.tile([P, PAIR_COLS // 4], U8, align_bytes=64, name="w2_scales")
                nc.vector.quantize_mx(
                    out=codes2[:].bitcast(FP8X4), scales=scales2[:], in_=w_squared[pair][:]
                )
                codes = w_work.tile([P, PAIR_COLS // 4], U32, align_bytes=64, name="w_codes")
                scales = w_work.tile([P, PAIR_COLS // 4], U8, align_bytes=64, name="w_scales")
                nc.vector.quantize_mx(
                    out=codes[:].bitcast(FP8X4), scales=scales[:], in_=w_grouped[pair][:]
                )
                w_codes[pair] = codes
                w_scales[pair] = scales
                w2_codes[pair] = codes2
                w2_scales[pair] = scales2

            def multiply_into(banks, product, moving_codes, moving_scales, pair):
                for gl in range(PAIR):
                    g = (pair * PAIR + gl) % PASSES
                    moving = slice(gl * ROUND_OUT, (gl + 1) * ROUND_OUT)
                    for a in range(TOKEN_TILES):
                        first = (2 * g + product) * TOKENS + a * P
                        nc.tensor.matmul_mx(
                            out=banks[a][:],
                            lhsT=prod_codes[:, first : first + P].bitcast(FP8X4),
                            lhsT_scale=prod_scales[:, first : first + P],
                            rhs=moving_codes[:, moving].bitcast(FP8X4),
                            rhs_scale=moving_scales[:, moving],
                            start=(g == 0),
                            stop=(g == PASSES - 1),
                        )

            def multiply(pair):
                if pair % ROUND_PAIRS == 0:
                    for a in range(TOKEN_TILES):
                        y_bank = sums.tile([P, BANK], F32, name="y_bank%d" % a)
                        q_bank = sums.tile([P, BANK], F32, name="q_bank%d" % a, bufs=2)
                        y_sums[a] = y_bank
                        q_sums[a] = q_bank
                multiply_into(q_sums, 1, w2_codes[pair], w2_scales[pair], pair)
                multiply_into(y_sums, 0, w_codes[pair], w_scales[pair], pair)

            def finish_round(h):
                results = []
                for a in range(TOKEN_TILES):
                    demod = tail.tile([P, ROUND_OUT], F32)
                    nc.scalar.activation(
                        out=demod[:], in_=q_sums[a][:], func=ACT.Abs_reciprocal_sqrt, bias=eps[:]
                    )
                    result = tail.tile([P, ROUND_OUT], F32)
                    nc.vector.tensor_tensor(out=result[:], in0=y_sums[a][:], in1=demod[:], op=ALU.mult)
                    results.append(result)
                for a in range(TOKEN_TILES):
                    nc.vector.tensor_tensor(
                        out=results[a][:], in0=results[a][:],
                        in1=bias_all[:, h * ROUND_OUT : (h + 1) * ROUND_OUT], op=ALU.add,
                    )
                    nc.sync.dma_start(
                        out=out_rows[a * P : (a + 1) * P, h * ROUND_OUT : (h + 1) * ROUND_OUT],
                        in_=results[a][:],
                    )

            square(0)
            for b in range(W_PAIRS + 1):
                issue_weight_load(STAGE1_TURNS + b + AHEAD)
                if b == ROUND_PAIRS + 1:
                    finish_round(0)
                if b + 1 < W_PAIRS:
                    square(b + 1)
                if b < W_PAIRS:
                    quantise(b)
                if W_EARLY + b < W_PASSES:
                    turn_weight(W_EARLY + b)
                if b >= 1:
                    multiply(b - 1)
            finish_round(1)
